import numpy as np
import ml_dtypes


def mxq(x, axis, fmt="e4m3"):
    dtype, down = {"e4m3": (ml_dtypes.float8_e4m3fn, 7), "e5m2": (ml_dtypes.float8_e5m2, 14)}[fmt]
    v = np.moveaxis(np.asarray(x, np.float32).astype(ml_dtypes.bfloat16).astype(np.float64), axis, -1)
    blocks = v.reshape(v.shape[:-1] + (-1, 32))
    amax = np.abs(blocks).max(-1, keepdims=True)
    byte = np.maximum(np.where(amax > 0, np.frexp(amax)[1] - 1 + 127, 0) - down, 1)
    scale = np.exp2(byte - 127.0)
    codes = (blocks / scale).astype(np.float32).astype(dtype).astype(np.float64)
    return np.moveaxis((codes * scale).reshape(v.shape), -1, axis)


WIDE = False


def mx_kscale(k):
    if not WIDE:
        return np.ones(k)
    levels = np.array([10, -10, 5, -5, 0])
    a = np.random.permutation(np.resize(levels, k // 512 * 4)).reshape(k // 512, 4)
    idx = np.arange(k)
    return np.exp2(a[idx // 512, idx % 128 // 32])


BF16 = ml_dtypes.bfloat16


def bf(x):
    return np.asarray(x, np.float32).astype(BF16)


def f64(x):
    return np.asarray(x).astype(np.float64)


L, P, B, H = 4, 2, 512, 1536
KEEP_PROB = 0.7


def setup_inputs():
    s = mx_kscale(H)
    w = np.random.standard_normal((P, H, H)) / np.sqrt(H)
    w[0] = w[0] / s[None, :]
    return {"h_in": bf(np.random.standard_normal((B, H)) * 1.3 * s),
            "w": bf(w),
            "masks": bf(np.random.uniform(size=(P, H, H)) < KEEP_PROB),
            "mu": bf(np.random.uniform(-0.5, 0.5, (P, H))),
            "sigma": bf(np.random.uniform(0.05, 0.5, (P, H))),
            "z": bf(np.random.standard_normal((P, B, H)))}


def reference(h_in, w, masks, mu, sigma, z):
    h, w, masks, mu, sigma, z = f64(h_in), f64(w), f64(masks), f64(mu), f64(sigma), f64(z)
    acts = []
    for l in range(P):
        wm_t = (w[l] * masks[l]).T
        pre = mxq(h, 1, "e4m3") @ mxq(wm_t, 0, "e4m3")
        noise = np.exp(mu[l][None, :] + sigma[l][None, :] * z[l])
        h = np.maximum(pre + noise, 0.0)
        acts.append(h)
    return np.concatenate(acts, axis=1)

@@ -1,0 +1,259 @@
+from contextlib import ExitStack
+
+import concourse.masks as masks_lib
+import concourse.mybir as mybir
+
+F32 = mybir.dt.float32
+BF16 = mybir.dt.bfloat16
+U32 = mybir.dt.uint32
+U8 = mybir.dt.uint8
+FP8X4 = mybir.dt.float8_e4m3fn_x4
+FUNC = mybir.ActivationFunctionType
+ALU = mybir.AluOpType
+
+P = 128
+LAYERS = 2
+ROWS = 512
+ROW_TILES = ROWS // P
+FEATURES = 1536
+K_PASS = 4 * P
+PASSES = FEATURES // K_PASS
+GROUP = 2 * P
+GROUPS = FEATURES // GROUP
+STEPS = LAYERS * GROUPS
+AHEAD = 6
+
+FLOPS = 2 * LAYERS * ROWS * FEATURES * FEATURES
+
+
+def tile_scm_mlp_pa_kernel(tc, h_in, w, masks, mu, sigma, z, out):
+    nc = tc.nc
+
+    h_view = h_in.rearrange("(r q) k -> q r k", q=P)
+    w_view = w.rearrange("l (u p e) k -> l u p e k", p=P, e=2)
+    m_view = masks.rearrange("l (u p e) k -> l u p e k", p=P, e=2)
+    z_view = z.rearrange("l (r q) f -> l q r f", q=P)
+    out_view = out.rearrange("(r q) f -> q r f", q=P)
+
+    with ExitStack() as ctx:
+        ctx.enter_context(tc.manual_schedule())
+        keep = ctx.enter_context(tc.tile_pool(name="keep", bufs=1))
+        z_pool = ctx.enter_context(tc.tile_pool(name="z", bufs=LAYERS))
+        w_pool = ctx.enter_context(tc.tile_pool(name="w", bufs=AHEAD))
+        grouped_pool = ctx.enter_context(tc.tile_pool(name="grouped", bufs=2))
+        codes_pool = ctx.enter_context(tc.tile_pool(name="codes", bufs=3))
+        noise_pool = ctx.enter_context(tc.tile_pool(name="noise", bufs=3))
+        sums_pool = ctx.enter_context(tc.tile_pool(name="sums", bufs=3))
+        result_pool = ctx.enter_context(tc.tile_pool(name="result", bufs=3))
+        turned_psum = ctx.enter_context(tc.psum_pool(name="turned", bufs=PASSES))
+        z_psum = ctx.enter_context(tc.psum_pool(name="z_turned", bufs=1))
+        acc_psum = ctx.enter_context(tc.psum_pool(name="acc", bufs=2))
+        back_psum = ctx.enter_context(tc.psum_pool(name="back", bufs=2))
+
+        identity = keep.tile([P, P], F32)
+        masks_lib.make_identity(nc, identity[:])
+
+
+        def turn_block(block):
+            banks = []
+            for g in range(PASSES):
+                bank = turned_psum.tile([P, 2, 2, P], F32)
+                for half in range(2):
+                    first_word = (K_PASS // 2) * g + P * half
+                    for e in range(2):
+                        nc.tensor.transpose(
+                            out=bank[:, half, e, :],
+                            in_=block[:, e, :].bitcast(F32)[:, first_word : first_word + P],
+                            identity=identity[:],
+                        )
+                banks.append(bank)
+            return banks
+
+        def regroup_block(banks):
+            grouped = grouped_pool.tile([P, PASSES, 4 * GROUP], BF16, align_bytes=64)
+            for g in range(PASSES):
+                nc.scalar.copy(
+                    out=grouped[:, g, :].bitcast(F32).rearrange("p (c half) -> p c half", half=2),
+                    in_=banks[g][:].rearrange("p half e c -> p (e c) half"),
+                )
+            return grouped
+
+        def quantise_block(grouped, codes, scales, columns):
+            for g in range(PASSES):
+                nc.vector.quantize_mx(
+                    out=codes[:, g, columns].bitcast(FP8X4),
+                    scales=scales[:, g, columns],
+                    in_=grouped[:, g, :],
+                )
+
+        rows = keep.tile([P, GROUP], BF16)
+        nc.vector.memset(rows[:], 0.0)
+
+        h_sb = keep.tile([P, ROW_TILES, FEATURES], BF16)
+        for b in range(ROW_TILES // 2):
+            nc.sync.dma_start(out=h_sb[:, 2 * b : 2 * b + 2, :], in_=h_view[:, 2 * b : 2 * b + 2, :])
+        nc.sync.dma_start(out=rows[0:STEPS, :], in_=mu.rearrange("l (u f) -> (l u) f", f=GROUP))
+        nc.sync.dma_start(
+            out=rows[STEPS : 2 * STEPS, :], in_=sigma.rearrange("l (u f) -> (l u) f", f=GROUP)
+        )
+
+        w_sb = {}
+        m_sb = {}
+        z_sb = {}
+
+        def load(i):
+            layer, u = divmod(i, GROUPS)
+            w_sb[i] = w_pool.tile([P, 2, FEATURES], BF16, name="w_sb")
+            nc.sync.dma_start(out=w_sb[i][:], in_=w_view[layer, u])
+            m_sb[i] = w_pool.tile([P, 2, FEATURES], BF16, name="m_sb")
+            nc.sync.dma_start(out=m_sb[i][:], in_=m_view[layer, u])
+            if u == 0:
+                z_sb[layer] = z_pool.tile([P, ROW_TILES, FEATURES], BF16, name="z_sb")
+                nc.sync.dma_start(out=z_sb[layer][:], in_=z_view[layer])
+
+        act_codes = []
+        act_scales = []
+        for layer in range(LAYERS):
+            act_codes.append(
+                keep.tile([P, PASSES, ROWS], U32, name="act_codes%d" % layer, align_bytes=64)
+            )
+            act_scales.append(
+                keep.tile([P, PASSES, ROWS], U8, name="act_scales%d" % layer, align_bytes=64)
+            )
+        for b in range(ROW_TILES // 2):
+            h_grouped = regroup_block(turn_block(h_sb[:, 2 * b : 2 * b + 2, :]))
+            quantise_block(h_grouped, act_codes[0], act_scales[0], slice(2 * P * b, 2 * P * (b + 1)))
+
+        rows_bank = z_psum.tile([P, ROWS], F32, name="z_bank")
+        nc.tensor.transpose(out=rows_bank[:, 0:P], in_=rows[:].bitcast(F32), identity=identity[:])
+        table = keep.tile([P, 4 * STEPS], F32)
+        nc.vector.tensor_copy(out=table[:], in_=rows_bank[:, 0 : 2 * STEPS].bitcast(BF16))
+
+        turned = {}
+        w_grouped = {}
+        w_codes = {}
+        w_scales = {}
+        z_bank = {}
+        noise = {}
+        acc = {}
+        sums = {}
+        back = {}
+
+        def mask_weights(i):
+            nc.vector.tensor_tensor(out=w_sb[i][:], in0=w_sb[i][:], in1=m_sb[i][:], op=ALU.mult)
+
+        def turn_weights(i):
+            turned[i] = turn_block(w_sb[i])
+
+        def regroup_weights(i):
+            w_grouped[i] = regroup_block(turned[i])
+
+        def quantise_weights(i):
+            w_codes[i] = codes_pool.tile([P, PASSES, GROUP], U32, name="w_codes", align_bytes=64)
+            w_scales[i] = codes_pool.tile([P, PASSES, GROUP], U8, name="w_scales", align_bytes=64)
+            quantise_block(w_grouped[i], w_codes[i], w_scales[i], slice(0, GROUP))
+
+        def multiply(i):
+            layer = i // GROUPS
+            acc[i] = []
+            for e in range(2):
+                bank = acc_psum.tile([P, ROWS], F32, name="acc")
+                tile_columns = slice(P * e, P * (e + 1))
+                for g in range(PASSES):
+                    nc.tensor.matmul_mx(
+                        out=bank[:],
+                        lhsT=w_codes[i][:, g, tile_columns].bitcast(FP8X4),
+                        lhsT_scale=w_scales[i][:, g, tile_columns],
+                        rhs=act_codes[layer][:, g, :].bitcast(FP8X4),
+                        rhs_scale=act_scales[layer][:, g, :],
+                        start=(g == 0),
+                        stop=(g == PASSES - 1),
+                    )
+                acc[i].append(bank)
+
+        def turn_z(i):
+            layer, u = divmod(i, GROUPS)
+            z_bank[i] = z_psum.tile([P, ROWS], F32, name="z_bank")
+            for r in range(ROW_TILES):
+                nc.tensor.transpose(
+                    out=z_bank[i][:, P * r : P * (r + 1)],
+                    in_=z_sb[layer][:, r, :].bitcast(F32)[:, P * u : P * (u + 1)],
+                    identity=identity[:],
+                )
+
+        def make_noise(i):
+            noise[i] = noise_pool.tile([P, 2, ROWS], F32, name="noise")
+            z_pairs = z_bank[i][:].bitcast(BF16).rearrange("p (n e) -> p n e", e=2)
+            for e in range(2):
+                nc.scalar.activation(
+                    out=noise[i][:, e, :],
+                    in_=z_pairs[:, :, e],
+                    func=FUNC.Exp,
+                    bias=table[:, 2 * i + e : 2 * i + e + 1],
+                    scale=table[:, 2 * (STEPS + i) + e : 2 * (STEPS + i) + e + 1],
+                )
+
+        def add_noise(i):
+            layer, u = divmod(i, GROUPS)
+            pair = i // 2
+            if u % 2 == 0:
+                sums[pair] = sums_pool.tile([P, 4, ROWS], F32, name="sums")
+            for e in range(2):
+                nc.vector.tensor_tensor(
+                    out=sums[pair][:, 2 * (u % 2) + e, :],
+                    in0=acc[i][e][:],
+                    in1=noise[i][:, e, :],
+                    op=ALU.add,
+                )
+            if layer == 0 and u % 2 == 1:
+                a_grouped = grouped_pool.tile([P, ROWS, 4], BF16, name="a_grouped", align_bytes=64)
+                nc.vector.tensor_scalar_max(
+                    out=a_grouped[:], in0=sums[pair][:].rearrange("p t n -> p n t"), scalar1=0.0
+                )
+                nc.vector.quantize_mx(
+                    out=act_codes[1][:, u // 2, :].bitcast(FP8X4),
+                    scales=act_scales[1][:, u // 2, :],
+                    in_=a_grouped[:].rearrange("p n t -> p (n t)"),
+                )
+
+        def turn_back(i):
+            u = i % GROUPS
+            back[i] = []
+            for b in range(ROW_TILES // 2):
+                bank = back_psum.tile([P, 2, 2, P], F32, name="back")
+                for r in range(2):
+                    first_row = P * (2 * b + r)
+                    for e in range(2):
+                        nc.tensor.transpose(
+                            out=bank[:, r, e, :],
+                            in_=sums[i // 2][:, 2 * (u % 2) + e, first_row : first_row + P],
+                            identity=identity[:],
+                        )
+                back[i].append(bank)
+
+        def store(i):
+            result = result_pool.tile([P, ROW_TILES, GROUP], F32)
+            for b in range(ROW_TILES // 2):
+                nc.scalar.activation(
+                    out=result[:, 2 * b : 2 * b + 2, :].rearrange("q r (p e) -> q r p e", e=2),
+                    in_=back[i][b][:].rearrange("q r e p -> q r p e"),
+                    func=FUNC.Relu,
+                )
+            nc.scalar.dma_start(out=out_view[:, :, GROUP * i : GROUP * (i + 1)], in_=result[:])
+
+        def stage(work, i):
+            if 0 <= i < STEPS:
+                work(i)
+
+        for step in range(-AHEAD, STEPS + 2):
+            stage(mask_weights, step + 1)
+            stage(turn_weights, step)
+            stage(regroup_weights, step)
+            stage(quantise_weights, step)
+            stage(multiply, step - 1)
+            stage(add_noise, step - 1)
+            stage(turn_back, step - 2)
+            stage(turn_z, step)
+            stage(store, step - 2)
+            stage(make_noise, step)
+            stage(load, step + AHEAD)

@@ -22,6 +22,8 @@ GROUP = 2 * P
 GROUPS = FEATURES // GROUP
 STEPS = LAYERS * GROUPS
 AHEAD = 6
+Z_PARTS = 2
+Z_GROUPS = GROUPS // Z_PARTS
 
 FLOPS = 2 * LAYERS * ROWS * FEATURES * FEATURES
 
@@ -38,7 +40,7 @@ def tile_scm_mlp_pa_kernel(tc, h_in, w, masks, mu, sigma, z, out):
     with ExitStack() as ctx:
         ctx.enter_context(tc.manual_schedule())
         keep = ctx.enter_context(tc.tile_pool(name="keep", bufs=1))
-        z_pool = ctx.enter_context(tc.tile_pool(name="z", bufs=LAYERS))
+        z_pool = ctx.enter_context(tc.tile_pool(name="z", bufs=LAYERS * Z_PARTS))
         w_pool = ctx.enter_context(tc.tile_pool(name="w", bufs=AHEAD))
         grouped_pool = ctx.enter_context(tc.tile_pool(name="grouped", bufs=2))
         codes_pool = ctx.enter_context(tc.tile_pool(name="codes", bufs=3))
@@ -107,9 +109,10 @@ def tile_scm_mlp_pa_kernel(tc, h_in, w, masks, mu, sigma, z, out):
             nc.sync.dma_start(out=w_sb[i][:], in_=w_view[layer, u])
             m_sb[i] = w_pool.tile([P, 2, FEATURES], BF16, name="m_sb")
             nc.sync.dma_start(out=m_sb[i][:], in_=m_view[layer, u])
-            if u == 0:
-                z_sb[layer] = z_pool.tile([P, ROW_TILES, FEATURES], BF16, name="z_sb")
-                nc.sync.dma_start(out=z_sb[layer][:], in_=z_view[layer])
+            if u % Z_GROUPS == 0:
+                z_columns = slice(GROUP * u, GROUP * (u + Z_GROUPS))
+                z_sb[i] = z_pool.tile([P, ROW_TILES, GROUP * Z_GROUPS], BF16, name="z_sb")
+                nc.sync.dma_start(out=z_sb[i][:], in_=z_view[layer][:, :, z_columns])
 
         act_codes = []
         act_scales = []
@@ -172,12 +175,12 @@ def tile_scm_mlp_pa_kernel(tc, h_in, w, masks, mu, sigma, z, out):
                 acc[i].append(bank)
 
         def turn_z(i):
-            layer, u = divmod(i, GROUPS)
+            place = i % Z_GROUPS
             z_bank[i] = z_psum.tile([P, ROWS], F32, name="z_bank")
             for r in range(ROW_TILES):
                 nc.tensor.transpose(
                     out=z_bank[i][:, P * r : P * (r + 1)],
-                    in_=z_sb[layer][:, r, :].bitcast(F32)[:, P * u : P * (u + 1)],
+                    in_=z_sb[i - place][:, r, :].bitcast(F32)[:, P * place : P * (place + 1)],
                     identity=identity[:],
                 )
 
@@ -245,15 +248,15 @@ def tile_scm_mlp_pa_kernel(tc, h_in, w, masks, mu, sigma, z, out):
             if 0 <= i < STEPS:
                 work(i)
 
-        for step in range(-AHEAD, STEPS + 2):
-            stage(mask_weights, step + 1)
+        for step in range(-AHEAD, STEPS + 1):
             stage(turn_weights, step)
+            stage(add_noise, step - 1)
             stage(regroup_weights, step)
             stage(quantise_weights, step)
-            stage(multiply, step - 1)
-            stage(add_noise, step - 1)
-            stage(turn_back, step - 2)
+            stage(turn_back, step - 1)
             stage(turn_z, step)
-            stage(store, step - 2)
+            stage(store, step - 1)
             stage(make_noise, step)
+            stage(mask_weights, step + 1)
+            stage(multiply, step)
             stage(load, step + AHEAD)

@@ -56,20 +56,17 @@ def tile_scm_mlp_pa_kernel(tc, h_in, w, masks, mu, sigma, z, out):
         masks_lib.make_identity(nc, identity[:])
 
 
-        def turn_block(block):
-            banks = []
-            for g in range(PASSES):
-                bank = turned_psum.tile([P, 2, 2, P], F32)
-                for half in range(2):
-                    first_word = (K_PASS // 2) * g + P * half
-                    for e in range(2):
-                        nc.tensor.transpose(
-                            out=bank[:, half, e, :],
-                            in_=block[:, e, :].bitcast(F32)[:, first_word : first_word + P],
-                            identity=identity[:],
-                        )
-                banks.append(bank)
-            return banks
+        def turn_pass(block, g):
+            bank = turned_psum.tile([P, 2, 2, P], F32)
+            for half in range(2):
+                first_word = (K_PASS // 2) * g + P * half
+                for e in range(2):
+                    nc.tensor.transpose(
+                        out=bank[:, half, e, :],
+                        in_=block[:, e, :].bitcast(F32)[:, first_word : first_word + P],
+                        identity=identity[:],
+                    )
+            return bank
 
         def regroup_block(banks):
             grouped = grouped_pool.tile([P, PASSES, 4 * GROUP], BF16, align_bytes=64)
@@ -124,7 +121,8 @@ def tile_scm_mlp_pa_kernel(tc, h_in, w, masks, mu, sigma, z, out):
                 keep.tile([P, PASSES, ROWS], U8, name="act_scales%d" % layer, align_bytes=64)
             )
         for b in range(ROW_TILES // 2):
-            h_grouped = regroup_block(turn_block(h_sb[:, 2 * b : 2 * b + 2, :]))
+            h_block = h_sb[:, 2 * b : 2 * b + 2, :]
+            h_grouped = regroup_block([turn_pass(h_block, g) for g in range(PASSES)])
             quantise_block(h_grouped, act_codes[0], act_scales[0], slice(2 * P * b, 2 * P * (b + 1)))
 
         rows_bank = z_psum.tile([P, ROWS], F32, name="z_bank")
@@ -145,34 +143,32 @@ def tile_scm_mlp_pa_kernel(tc, h_in, w, masks, mu, sigma, z, out):
         def mask_weights(i):
             nc.vector.tensor_tensor(out=w_sb[i][:], in0=w_sb[i][:], in1=m_sb[i][:], op=ALU.mult)
 
-        def turn_weights(i):
-            turned[i] = turn_block(w_sb[i])
+        def turn_weights(i, first_pass, end_pass):
+            for g in range(first_pass, end_pass):
+                turned[i, g] = turn_pass(w_sb[i], g)
 
         def regroup_weights(i):
-            w_grouped[i] = regroup_block(turned[i])
+            w_grouped[i] = regroup_block([turned[i, g] for g in range(PASSES)])
 
         def quantise_weights(i):
             w_codes[i] = codes_pool.tile([P, PASSES, GROUP], U32, name="w_codes", align_bytes=64)
             w_scales[i] = codes_pool.tile([P, PASSES, GROUP], U8, name="w_scales", align_bytes=64)
             quantise_block(w_grouped[i], w_codes[i], w_scales[i], slice(0, GROUP))
 
-        def multiply(i):
+        def multiply(i, e):
             layer = i // GROUPS
-            acc[i] = []
-            for e in range(2):
-                bank = acc_psum.tile([P, ROWS], F32, name="acc")
-                tile_columns = slice(P * e, P * (e + 1))
-                for g in range(PASSES):
-                    nc.tensor.matmul_mx(
-                        out=bank[:],
-                        lhsT=w_codes[i][:, g, tile_columns].bitcast(FP8X4),
-                        lhsT_scale=w_scales[i][:, g, tile_columns],
-                        rhs=act_codes[layer][:, g, :].bitcast(FP8X4),
-                        rhs_scale=act_scales[layer][:, g, :],
-                        start=(g == 0),
-                        stop=(g == PASSES - 1),
-                    )
-                acc[i].append(bank)
+            acc[i, e] = acc_psum.tile([P, ROWS], F32, name="acc")
+            tile_columns = slice(P * e, P * (e + 1))
+            for g in range(PASSES):
+                nc.tensor.matmul_mx(
+                    out=acc[i, e][:],
+                    lhsT=w_codes[i][:, g, tile_columns].bitcast(FP8X4),
+                    lhsT_scale=w_scales[i][:, g, tile_columns],
+                    rhs=act_codes[layer][:, g, :].bitcast(FP8X4),
+                    rhs_scale=act_scales[layer][:, g, :],
+                    start=(g == 0),
+                    stop=(g == PASSES - 1),
+                )
 
         def turn_z(i):
             place = i % Z_GROUPS
@@ -204,7 +200,7 @@ def tile_scm_mlp_pa_kernel(tc, h_in, w, masks, mu, sigma, z, out):
             for e in range(2):
                 nc.vector.tensor_tensor(
                     out=sums[pair][:, 2 * (u % 2) + e, :],
-                    in0=acc[i][e][:],
+                    in0=acc[i, e][:],
                     in1=noise[i][:, e, :],
                     op=ALU.add,
                 )
@@ -244,19 +240,21 @@ def tile_scm_mlp_pa_kernel(tc, h_in, w, masks, mu, sigma, z, out):
                 )
             nc.scalar.dma_start(out=out_view[:, :, GROUP * i : GROUP * (i + 1)], in_=result[:])
 
-        def stage(work, i):
+        def stage(work, i, *more):
             if 0 <= i < STEPS:
-                work(i)
+                work(i, *more)
 
-        for step in range(-AHEAD, STEPS + 1):
-            stage(turn_weights, step)
-            stage(add_noise, step - 1)
+        for step in range(-AHEAD, STEPS + 2):
+            stage(mask_weights, step + 1)
+            stage(turn_weights, step, 0, 2)
+            stage(multiply, step - 1, 0)
+            stage(turn_weights, step, 2, PASSES)
+            stage(turn_z, step)
+            stage(multiply, step - 1, 1)
+            stage(turn_back, step - 2)
             stage(regroup_weights, step)
             stage(quantise_weights, step)
-            stage(turn_back, step - 1)
-            stage(turn_z, step)
-            stage(store, step - 1)
+            stage(add_noise, step - 1)
             stage(make_noise, step)
-            stage(mask_weights, step + 1)
-            stage(multiply, step)
+            stage(store, step - 2)
             stage(load, step + AHEAD)

@@ -46,7 +46,7 @@ def tile_scm_mlp_pa_kernel(tc, h_in, w, masks, mu, sigma, z, out):
         codes_pool = ctx.enter_context(tc.tile_pool(name="codes", bufs=3))
         noise_pool = ctx.enter_context(tc.tile_pool(name="noise", bufs=3))
         sums_pool = ctx.enter_context(tc.tile_pool(name="sums", bufs=3))
-        result_pool = ctx.enter_context(tc.tile_pool(name="result", bufs=3))
+        result_pool = ctx.enter_context(tc.tile_pool(name="result", bufs=5))
         turned_psum = ctx.enter_context(tc.psum_pool(name="turned", bufs=PASSES))
         z_psum = ctx.enter_context(tc.psum_pool(name="z_turned", bufs=1))
         acc_psum = ctx.enter_context(tc.psum_pool(name="acc", bufs=2))
@@ -238,7 +238,7 @@ def tile_scm_mlp_pa_kernel(tc, h_in, w, masks, mu, sigma, z, out):
                     in_=back[i][b][:].rearrange("q r e p -> q r p e"),
                     func=FUNC.Relu,
                 )
-            nc.scalar.dma_start(out=out_view[:, :, GROUP * i : GROUP * (i + 1)], in_=result[:])
+            nc.sync.dma_start(out=out_view[:, :, GROUP * i : GROUP * (i + 1)], in_=result[:])
 
         def stage(work, i, *more):
             if 0 <= i < STEPS:

@@ -21,7 +21,7 @@ PASSES = FEATURES // K_PASS
 GROUP = 2 * P
 GROUPS = FEATURES // GROUP
 STEPS = LAYERS * GROUPS
-AHEAD = 6
+SLOTS = 8
 Z_PARTS = 2
 Z_GROUPS = GROUPS // Z_PARTS
 
@@ -41,76 +41,66 @@ def tile_scm_mlp_pa_kernel(tc, h_in, w, masks, mu, sigma, z, out):
         ctx.enter_context(tc.manual_schedule())
         keep = ctx.enter_context(tc.tile_pool(name="keep", bufs=1))
         z_pool = ctx.enter_context(tc.tile_pool(name="z", bufs=LAYERS * Z_PARTS))
-        w_pool = ctx.enter_context(tc.tile_pool(name="w", bufs=AHEAD))
+        w_pool = ctx.enter_context(tc.tile_pool(name="w", bufs=SLOTS))
         grouped_pool = ctx.enter_context(tc.tile_pool(name="grouped", bufs=2))
         codes_pool = ctx.enter_context(tc.tile_pool(name="codes", bufs=3))
         noise_pool = ctx.enter_context(tc.tile_pool(name="noise", bufs=3))
         sums_pool = ctx.enter_context(tc.tile_pool(name="sums", bufs=3))
-        result_pool = ctx.enter_context(tc.tile_pool(name="result", bufs=5))
-        turned_psum = ctx.enter_context(tc.psum_pool(name="turned", bufs=PASSES))
+        result_pool = ctx.enter_context(tc.tile_pool(name="result", bufs=3))
+        turned_psum = ctx.enter_context(tc.psum_pool(name="turned", bufs=2))
         z_psum = ctx.enter_context(tc.psum_pool(name="z_turned", bufs=1))
-        acc_psum = ctx.enter_context(tc.psum_pool(name="acc", bufs=2))
+        acc_psum = ctx.enter_context(tc.psum_pool(name="acc", bufs=3))
         back_psum = ctx.enter_context(tc.psum_pool(name="back", bufs=2))
 
         identity = keep.tile([P, P], F32)
         masks_lib.make_identity(nc, identity[:])
 
-
-        def turn_pass(block, g):
-            bank = turned_psum.tile([P, 2, 2, P], F32)
-            for half in range(2):
-                first_word = (K_PASS // 2) * g + P * half
-                for e in range(2):
-                    nc.tensor.transpose(
-                        out=bank[:, half, e, :],
-                        in_=block[:, e, :].bitcast(F32)[:, first_word : first_word + P],
-                        identity=identity[:],
-                    )
-            return bank
-
-        def regroup_block(banks):
-            grouped = grouped_pool.tile([P, PASSES, 4 * GROUP], BF16, align_bytes=64)
-            for g in range(PASSES):
-                nc.scalar.copy(
-                    out=grouped[:, g, :].bitcast(F32).rearrange("p (c half) -> p c half", half=2),
-                    in_=banks[g][:].rearrange("p half e c -> p (e c) half"),
-                )
-            return grouped
-
-        def quantise_block(grouped, codes, scales, columns):
-            for g in range(PASSES):
-                nc.vector.quantize_mx(
-                    out=codes[:, g, columns].bitcast(FP8X4),
-                    scales=scales[:, g, columns],
-                    in_=grouped[:, g, :],
-                )
-
         rows = keep.tile([P, GROUP], BF16)
         nc.vector.memset(rows[:], 0.0)
-
-        h_sb = keep.tile([P, ROW_TILES, FEATURES], BF16)
-        for b in range(ROW_TILES // 2):
-            nc.sync.dma_start(out=h_sb[:, 2 * b : 2 * b + 2, :], in_=h_view[:, 2 * b : 2 * b + 2, :])
-        nc.sync.dma_start(out=rows[0:STEPS, :], in_=mu.rearrange("l (u f) -> (l u) f", f=GROUP))
-        nc.sync.dma_start(
-            out=rows[STEPS : 2 * STEPS, :], in_=sigma.rearrange("l (u f) -> (l u) f", f=GROUP)
-        )
 
         w_sb = {}
         m_sb = {}
         z_sb = {}
+        h_sb = {}
 
-        def load(i):
+        def load_weights(i, halves=False):
             layer, u = divmod(i, GROUPS)
             w_sb[i] = w_pool.tile([P, 2, FEATURES], BF16, name="w_sb")
-            nc.sync.dma_start(out=w_sb[i][:], in_=w_view[layer, u])
             m_sb[i] = w_pool.tile([P, 2, FEATURES], BF16, name="m_sb")
-            nc.sync.dma_start(out=m_sb[i][:], in_=m_view[layer, u])
-            if u % Z_GROUPS == 0:
-                z_columns = slice(GROUP * u, GROUP * (u + Z_GROUPS))
-                z_sb[i] = z_pool.tile([P, ROW_TILES, GROUP * Z_GROUPS], BF16, name="z_sb")
-                nc.sync.dma_start(out=z_sb[i][:], in_=z_view[layer][:, :, z_columns])
+            parts = [slice(0, 1), slice(1, 2)] if halves else [slice(0, 2)]
+            for part in parts:
+                nc.sync.dma_start(out=w_sb[i][:, part, :], in_=w_view[layer, u][:, part, :])
+                nc.sync.dma_start(out=m_sb[i][:, part, :], in_=m_view[layer, u][:, part, :])
 
+        def load_h():
+            h_sb[0] = w_pool.tile([P, 2, FEATURES], BF16, name="w_sb")
+            h_sb[1] = w_pool.tile([P, 2, FEATURES], BF16, name="m_sb")
+            for b in range(2):
+                nc.sync.dma_start(out=h_sb[b][:], in_=h_view[:, 2 * b : 2 * b + 2, :])
+            nc.sync.dma_start(out=rows[0:STEPS, :], in_=mu.rearrange("l (u f) -> (l u) f", f=GROUP))
+            nc.sync.dma_start(
+                out=rows[STEPS : 2 * STEPS, :], in_=sigma.rearrange("l (u f) -> (l u) f", f=GROUP)
+            )
+
+        def load_z(part):
+            layer, half = divmod(part, Z_PARTS)
+            columns = GROUP * Z_GROUPS
+            z_sb[part] = z_pool.tile([P, ROW_TILES, columns], BF16, name="z_sb")
+            nc.sync.dma_start(
+                out=z_sb[part][:], in_=z_view[layer][:, :, columns * half : columns * (half + 1)]
+            )
+
+        turned = {}
+        grouped = {}
+        codes = {}
+        scales = {}
+        z_bank = {}
+        noise = {}
+        acc = {}
+        sums = {}
+        a_grouped = {}
+        back = {}
+        result = {}
         act_codes = []
         act_scales = []
         for layer in range(LAYERS):
@@ -120,63 +110,80 @@ def tile_scm_mlp_pa_kernel(tc, h_in, w, masks, mu, sigma, z, out):
             act_scales.append(
                 keep.tile([P, PASSES, ROWS], U8, name="act_scales%d" % layer, align_bytes=64)
             )
-        for b in range(ROW_TILES // 2):
-            h_block = h_sb[:, 2 * b : 2 * b + 2, :]
-            h_grouped = regroup_block([turn_pass(h_block, g) for g in range(PASSES)])
-            quantise_block(h_grouped, act_codes[0], act_scales[0], slice(2 * P * b, 2 * P * (b + 1)))
-
-        rows_bank = z_psum.tile([P, ROWS], F32, name="z_bank")
-        nc.tensor.transpose(out=rows_bank[:, 0:P], in_=rows[:].bitcast(F32), identity=identity[:])
         table = keep.tile([P, 4 * STEPS], F32)
-        nc.vector.tensor_copy(out=table[:], in_=rows_bank[:, 0 : 2 * STEPS].bitcast(BF16))
 
-        turned = {}
-        w_grouped = {}
-        w_codes = {}
-        w_scales = {}
-        z_bank = {}
-        noise = {}
-        acc = {}
-        sums = {}
-        back = {}
+        def mask_weights(i, part=slice(0, 2)):
+            nc.vector.tensor_tensor(
+                out=w_sb[i][:, part, :], in0=w_sb[i][:, part, :], in1=m_sb[i][:, part, :], op=ALU.mult
+            )
 
-        def mask_weights(i):
-            nc.vector.tensor_tensor(out=w_sb[i][:], in0=w_sb[i][:], in1=m_sb[i][:], op=ALU.mult)
+        def turn(key, block, g):
+            bank = turned_psum.tile([P, 2, 2, P], F32, name="turned")
+            for half in range(2):
+                first_word = (K_PASS // 2) * g + P * half
+                for e in range(2):
+                    nc.tensor.transpose(
+                        out=bank[:, half, e, :],
+                        in_=block[:, e, :].bitcast(F32)[:, first_word : first_word + P],
+                        identity=identity[:],
+                    )
+            turned[key, g] = bank
 
-        def turn_weights(i, first_pass, end_pass):
-            for g in range(first_pass, end_pass):
-                turned[i, g] = turn_pass(w_sb[i], g)
-
-        def regroup_weights(i):
-            w_grouped[i] = regroup_block([turned[i, g] for g in range(PASSES)])
-
-        def quantise_weights(i):
-            w_codes[i] = codes_pool.tile([P, PASSES, GROUP], U32, name="w_codes", align_bytes=64)
-            w_scales[i] = codes_pool.tile([P, PASSES, GROUP], U8, name="w_scales", align_bytes=64)
-            quantise_block(w_grouped[i], w_codes[i], w_scales[i], slice(0, GROUP))
-
-        def multiply(i, e):
-            layer = i // GROUPS
-            acc[i, e] = acc_psum.tile([P, ROWS], F32, name="acc")
-            tile_columns = slice(P * e, P * (e + 1))
-            for g in range(PASSES):
-                nc.tensor.matmul_mx(
-                    out=acc[i, e][:],
-                    lhsT=w_codes[i][:, g, tile_columns].bitcast(FP8X4),
-                    lhsT_scale=w_scales[i][:, g, tile_columns],
-                    rhs=act_codes[layer][:, g, :].bitcast(FP8X4),
-                    rhs_scale=act_scales[layer][:, g, :],
-                    start=(g == 0),
-                    stop=(g == PASSES - 1),
+        def regroup(key, g):
+            if g == 0:
+                grouped[key] = grouped_pool.tile(
+                    [P, PASSES, 4 * GROUP], BF16, name="grouped", align_bytes=64
                 )
+            nc.scalar.copy(
+                out=grouped[key][:, g, :].bitcast(F32).rearrange("p (c half) -> p c half", half=2),
+                in_=turned[key, g][:].rearrange("p half e c -> p (e c) half"),
+            )
+
+        def quantise_weights(i, g):
+            if g == 0:
+                codes[i] = codes_pool.tile([P, PASSES, GROUP], U32, name="codes", align_bytes=64)
+                scales[i] = codes_pool.tile([P, PASSES, GROUP], U8, name="scales", align_bytes=64)
+            nc.vector.quantize_mx(
+                out=codes[i][:, g, :].bitcast(FP8X4),
+                scales=scales[i][:, g, :],
+                in_=grouped[i][:, g, :],
+            )
+
+        def quantise_h(b, g):
+            columns = slice(2 * P * b, 2 * P * (b + 1))
+            nc.vector.quantize_mx(
+                out=act_codes[0][:, g, columns].bitcast(FP8X4),
+                scales=act_scales[0][:, g, columns],
+                in_=grouped["h", b][:, g, :],
+            )
+
+        def make_table():
+            bank = z_psum.tile([P, ROWS], F32, name="z_bank")
+            nc.tensor.transpose(out=bank[:, 0:P], in_=rows[:].bitcast(F32), identity=identity[:])
+            nc.vector.tensor_copy(out=table[:], in_=bank[:, 0 : 2 * STEPS].bitcast(BF16))
+
+        def multiply(i, e, g):
+            layer = i // GROUPS
+            if g == 0:
+                acc[i, e] = acc_psum.tile([P, ROWS], F32, name="acc")
+            tile_columns = slice(P * e, P * (e + 1))
+            nc.tensor.matmul_mx(
+                out=acc[i, e][:],
+                lhsT=codes[i][:, g, tile_columns].bitcast(FP8X4),
+                lhsT_scale=scales[i][:, g, tile_columns],
+                rhs=act_codes[layer][:, g, :].bitcast(FP8X4),
+                rhs_scale=act_scales[layer][:, g, :],
+                start=(g == 0),
+                stop=(g == PASSES - 1),
+            )
 
         def turn_z(i):
-            place = i % Z_GROUPS
+            part, place = divmod(i, Z_GROUPS)
             z_bank[i] = z_psum.tile([P, ROWS], F32, name="z_bank")
             for r in range(ROW_TILES):
                 nc.tensor.transpose(
                     out=z_bank[i][:, P * r : P * (r + 1)],
-                    in_=z_sb[i - place][:, r, :].bitcast(F32)[:, P * place : P * (place + 1)],
+                    in_=z_sb[part][:, r, :].bitcast(F32)[:, P * place : P * (place + 1)],
                     identity=identity[:],
                 )
 
@@ -192,69 +199,127 @@ def tile_scm_mlp_pa_kernel(tc, h_in, w, masks, mu, sigma, z, out):
                     scale=table[:, 2 * (STEPS + i) + e : 2 * (STEPS + i) + e + 1],
                 )
 
-        def add_noise(i):
-            layer, u = divmod(i, GROUPS)
-            pair = i // 2
-            if u % 2 == 0:
+        def add_noise(i, e):
+            pair, odd = divmod(i, 2)
+            if odd == 0 and e == 0:
                 sums[pair] = sums_pool.tile([P, 4, ROWS], F32, name="sums")
-            for e in range(2):
-                nc.vector.tensor_tensor(
-                    out=sums[pair][:, 2 * (u % 2) + e, :],
-                    in0=acc[i, e][:],
-                    in1=noise[i][:, e, :],
-                    op=ALU.add,
-                )
-            if layer == 0 and u % 2 == 1:
-                a_grouped = grouped_pool.tile([P, ROWS, 4], BF16, name="a_grouped", align_bytes=64)
-                nc.vector.tensor_scalar_max(
-                    out=a_grouped[:], in0=sums[pair][:].rearrange("p t n -> p n t"), scalar1=0.0
-                )
-                nc.vector.quantize_mx(
-                    out=act_codes[1][:, u // 2, :].bitcast(FP8X4),
-                    scales=act_scales[1][:, u // 2, :],
-                    in_=a_grouped[:].rearrange("p n t -> p (n t)"),
-                )
+            nc.vector.tensor_tensor(
+                out=sums[pair][:, 2 * odd + e, :], in0=acc[i, e][:], in1=noise[i][:, e, :], op=ALU.add
+            )
 
-        def turn_back(i):
-            u = i % GROUPS
-            back[i] = []
-            for b in range(ROW_TILES // 2):
-                bank = back_psum.tile([P, 2, 2, P], F32, name="back")
-                for r in range(2):
-                    first_row = P * (2 * b + r)
-                    for e in range(2):
-                        nc.tensor.transpose(
-                            out=bank[:, r, e, :],
-                            in_=sums[i // 2][:, 2 * (u % 2) + e, first_row : first_row + P],
-                            identity=identity[:],
-                        )
-                back[i].append(bank)
+        def round_a0(pair):
+            a_grouped[pair] = keep.tile([P, ROWS, 4], BF16, name="a_grouped", align_bytes=64)
+            nc.vector.tensor_scalar_max(
+                out=a_grouped[pair][:], in0=sums[pair][:].rearrange("p t n -> p n t"), scalar1=0.0
+            )
 
-        def store(i):
-            result = result_pool.tile([P, ROW_TILES, GROUP], F32)
-            for b in range(ROW_TILES // 2):
-                nc.scalar.activation(
-                    out=result[:, 2 * b : 2 * b + 2, :].rearrange("q r (p e) -> q r p e", e=2),
-                    in_=back[i][b][:].rearrange("q r e p -> q r p e"),
-                    func=FUNC.Relu,
-                )
-            nc.sync.dma_start(out=out_view[:, :, GROUP * i : GROUP * (i + 1)], in_=result[:])
+        def quantise_a0(pair):
+            nc.vector.quantize_mx(
+                out=act_codes[1][:, pair, :].bitcast(FP8X4),
+                scales=act_scales[1][:, pair, :],
+                in_=a_grouped[pair][:].rearrange("p n t -> p (n t)"),
+            )
 
-        def stage(work, i, *more):
+        def turn_back(i, b):
+            pair, odd = divmod(i, 2)
+            back[i, b] = back_psum.tile([P, 2, 2, P], F32, name="back")
+            for r in range(2):
+                first_row = P * (2 * b + r)
+                for e in range(2):
+                    nc.tensor.transpose(
+                        out=back[i, b][:, r, e, :],
+                        in_=sums[pair][:, 2 * odd + e, first_row : first_row + P],
+                        identity=identity[:],
+                    )
+
+        def finish(i, b):
+            pair, odd = divmod(i, 2)
+            if odd == 0 and b == 0:
+                result[pair] = result_pool.tile([P, ROW_TILES, 2 * GROUP], F32, name="result")
+            columns = slice(GROUP * odd, GROUP * (odd + 1))
+            nc.scalar.activation(
+                out=result[pair][:, 2 * b : 2 * b + 2, columns].rearrange(
+                    "q r (p e) -> q r p e", e=2
+                ),
+                in_=back[i, b][:].rearrange("q r e p -> q r p e"),
+                func=FUNC.Relu,
+            )
+
+        def store(pair, b):
+            nc.sync.dma_start(
+                out=out_view[:, 2 * b : 2 * b + 2, 2 * GROUP * pair : 2 * GROUP * (pair + 1)],
+                in_=result[pair][:, 2 * b : 2 * b + 2, :],
+            )
+
+        def load(i):
+            if i < STEPS:
+                load_weights(i)
+                if i % Z_GROUPS == 1:
+                    load_z(i // Z_GROUPS)
+
+        load_h()
+        for i in range(SLOTS - 1):
+            load(i)
+
+        for b in range(2):
+            for g in range(PASSES):
+                turn(("h", b), h_sb[b], g)
+                regroup(("h", b), g)
+            for g in range(PASSES):
+                quantise_h(b, g)
+        make_table()
+        mask_weights(0)
+
+        def turn_weights(i, passes):
+            if i < STEPS:
+                for g in passes:
+                    turn(i, w_sb[i], g)
+
+        def multiply_run(i, run):
             if 0 <= i < STEPS:
-                work(i, *more)
+                if i == GROUPS:
+                    order = (((0, 0), (0, 1), (1, 0)), ((1, 1), (0, 2), (1, 2)))[run]
+                else:
+                    order = [(run, g) for g in range(PASSES)]
+                for e, g in order:
+                    multiply(i, e, g)
 
-        for step in range(-AHEAD, STEPS + 2):
-            stage(mask_weights, step + 1)
-            stage(turn_weights, step, 0, 2)
-            stage(multiply, step - 1, 0)
-            stage(turn_weights, step, 2, PASSES)
-            stage(turn_z, step)
-            stage(multiply, step - 1, 1)
-            stage(turn_back, step - 2)
-            stage(regroup_weights, step)
-            stage(quantise_weights, step)
-            stage(add_noise, step - 1)
-            stage(make_noise, step)
-            stage(store, step - 2)
-            stage(load, step + AHEAD)
+        for step in range(STEPS + 2):
+            turn_weights(step, (0, 1))
+            multiply_run(step - 1, 0)
+            turn_weights(step, (2,))
+            if step < STEPS:
+                turn_z(step)
+            multiply_run(step - 1, 1)
+            if step >= 2:
+                for b in range(2):
+                    turn_back(step - 2, b)
+            if step == 0:
+                mask_weights(1)
+            if step < STEPS:
+                for g in range(PASSES):
+                    regroup(step, g)
+                for g in range(PASSES):
+                    quantise_weights(step, g)
+            late = step - 2 in (1, 3)
+            if late:
+                round_a0((step - 2) // 2)
+            if 1 <= step <= STEPS:
+                for e in range(2):
+                    add_noise(step - 1, e)
+            if late:
+                quantise_a0((step - 2) // 2)
+            if step == GROUPS:
+                round_a0(PASSES - 1)
+                quantise_a0(PASSES - 1)
+            if step + 2 < STEPS:
+                mask_weights(step + 2)
+            if step < STEPS:
+                make_noise(step)
+            if step >= 2:
+                for b in range(2):
+                    finish(step - 2, b)
+                if step % 2 == 1:
+                    for b in range(2):
+                        store((step - 2) // 2, b)
+            load(step + SLOTS - 1)

@@ -21,7 +21,7 @@ PASSES = FEATURES // K_PASS
 GROUP = 2 * P
 GROUPS = FEATURES // GROUP
 STEPS = LAYERS * GROUPS
-SLOTS = 8
+SLOTS = 7
 Z_PARTS = 2
 Z_GROUPS = GROUPS // Z_PARTS
 
@@ -31,11 +31,11 @@ FLOPS = 2 * LAYERS * ROWS * FEATURES * FEATURES
 def tile_scm_mlp_pa_kernel(tc, h_in, w, masks, mu, sigma, z, out):
     nc = tc.nc
 
-    h_view = h_in.rearrange("(r q) k -> q r k", q=P)
+    h_view = h_in.rearrange("(q r) k -> q r k", q=P)
     w_view = w.rearrange("l (u p e) k -> l u p e k", p=P, e=2)
     m_view = masks.rearrange("l (u p e) k -> l u p e k", p=P, e=2)
-    z_view = z.rearrange("l (r q) f -> l q r f", q=P)
-    out_view = out.rearrange("(r q) f -> q r f", q=P)
+    z_view = z.rearrange("l (q r) f -> l q r f", q=P)
+    out_view = out.rearrange("(q r) f -> q r f", q=P)
 
     with ExitStack() as ctx:
         ctx.enter_context(tc.manual_schedule())
@@ -44,7 +44,7 @@ def tile_scm_mlp_pa_kernel(tc, h_in, w, masks, mu, sigma, z, out):
         w_pool = ctx.enter_context(tc.tile_pool(name="w", bufs=SLOTS))
         grouped_pool = ctx.enter_context(tc.tile_pool(name="grouped", bufs=2))
         codes_pool = ctx.enter_context(tc.tile_pool(name="codes", bufs=3))
-        noise_pool = ctx.enter_context(tc.tile_pool(name="noise", bufs=3))
+        noise_pool = ctx.enter_context(tc.tile_pool(name="noise", bufs=5))
         sums_pool = ctx.enter_context(tc.tile_pool(name="sums", bufs=3))
         result_pool = ctx.enter_context(tc.tile_pool(name="result", bufs=3))
         turned_psum = ctx.enter_context(tc.psum_pool(name="turned", bufs=2))
@@ -222,7 +222,10 @@ def tile_scm_mlp_pa_kernel(tc, h_in, w, masks, mu, sigma, z, out):
 
         def turn_back(i, b):
             pair, odd = divmod(i, 2)
-            back[i, b] = back_psum.tile([P, 2, 2, P], F32, name="back")
+            if i == STEPS - 1:
+                back[i, b] = turned_psum.tile([P, 2, 2, P], F32, name="turned")
+            else:
+                back[i, b] = back_psum.tile([P, 2, 2, P], F32, name="back")
             for r in range(2):
                 first_row = P * (2 * b + r)
                 for e in range(2):
@@ -233,29 +236,39 @@ def tile_scm_mlp_pa_kernel(tc, h_in, w, masks, mu, sigma, z, out):
                     )
 
         def finish(i, b):
-            pair, odd = divmod(i, 2)
-            if odd == 0 and b == 0:
-                result[pair] = result_pool.tile([P, ROW_TILES, 2 * GROUP], F32, name="result")
-            columns = slice(GROUP * odd, GROUP * (odd + 1))
-            nc.scalar.activation(
-                out=result[pair][:, 2 * b : 2 * b + 2, columns].rearrange(
-                    "q r (p e) -> q r p e", e=2
-                ),
-                in_=back[i, b][:].rearrange("q r e p -> q r p e"),
-                func=FUNC.Relu,
+            odd = i % 2
+            if i >= STEPS - 2:
+                if b == 0:
+                    result[i] = result_pool.tile([P, ROW_TILES, GROUP], F32, name="result")
+                columns = slice(0, GROUP)
+            else:
+                if odd == 0 and b == 0:
+                    result[i] = result_pool.tile([P, ROW_TILES, 2 * GROUP], F32, name="result")
+                    result[i + 1] = result[i]
+                columns = slice(GROUP * odd, GROUP * (odd + 1))
+            target = result[i][:, 2 * b : 2 * b + 2, columns].rearrange(
+                "q r (p e) -> q r p e", e=2
+            )
+            source = back[i, b][:].rearrange("q r e p -> q r p e")
+            if i >= STEPS - 2 and b == 1:
+                nc.vector.tensor_scalar_max(out=target, in0=source, scalar1=0.0)
+            else:
+                nc.scalar.activation(out=target, in_=source, func=FUNC.Relu)
+
+        def store(i, halves):
+            first = i if i >= STEPS - 2 else i - 1
+            tiles = slice(2 * halves[0], 2 * halves[-1] + 2)
+            nc.sync.dma_start(
+                out=out_view[:, tiles, GROUP * first : GROUP * (i + 1)], in_=result[i][:, tiles, :]
             )
 
-        def store(pair, b):
-            nc.sync.dma_start(
-                out=out_view[:, 2 * b : 2 * b + 2, 2 * GROUP * pair : 2 * GROUP * (pair + 1)],
-                in_=result[pair][:, 2 * b : 2 * b + 2, :],
-            )
+        z_behind = {1: 0, 4: 1, 6: 2, 8: 3}
 
         def load(i):
             if i < STEPS:
                 load_weights(i)
-                if i % Z_GROUPS == 1:
-                    load_z(i // Z_GROUPS)
+                if i in z_behind:
+                    load_z(z_behind[i])
 
         load_h()
         for i in range(SLOTS - 1):
@@ -284,21 +297,28 @@ def tile_scm_mlp_pa_kernel(tc, h_in, w, masks, mu, sigma, z, out):
                 for e, g in order:
                     multiply(i, e, g)
 
+        z_done = 0
         for step in range(STEPS + 2):
+            z_end = min(STEPS, step + 1 + min(3, max(0, step - GROUPS + 2)))
+            z_now = range(z_done, z_end)
+            z_done = z_end
             turn_weights(step, (0, 1))
             multiply_run(step - 1, 0)
             turn_weights(step, (2,))
-            if step < STEPS:
-                turn_z(step)
-            multiply_run(step - 1, 1)
-            if step >= 2:
-                for b in range(2):
-                    turn_back(step - 2, b)
+            for i in z_now[:1]:
+                turn_z(i)
             if step == 0:
                 mask_weights(1)
             if step < STEPS:
                 for g in range(PASSES):
                     regroup(step, g)
+            for i in z_now[:1]:
+                make_noise(i)
+            multiply_run(step - 1, 1)
+            if step >= 2:
+                for b in range(2):
+                    turn_back(step - 2, b)
+            if step < STEPS:
                 for g in range(PASSES):
                     quantise_weights(step, g)
             late = step - 2 in (1, 3)
@@ -314,12 +334,16 @@ def tile_scm_mlp_pa_kernel(tc, h_in, w, masks, mu, sigma, z, out):
                 quantise_a0(PASSES - 1)
             if step + 2 < STEPS:
                 mask_weights(step + 2)
-            if step < STEPS:
-                make_noise(step)
             if step >= 2:
+                i = step - 2
                 for b in range(2):
-                    finish(step - 2, b)
-                if step % 2 == 1:
+                    finish(i, b)
+                if i == STEPS - 2:
+                    store(i, range(2))
+                elif i >= STEPS - 2 or i % 2 == 1:
                     for b in range(2):
-                        store((step - 2) // 2, b)
+                        store(i, range(b, b + 1))
+            for i in z_now[1:]:
+                turn_z(i)
+                make_noise(i)
             load(step + SLOTS - 1)

@@ -22,6 +22,8 @@ GROUP = 2 * P
 GROUPS = FEATURES // GROUP
 STEPS = LAYERS * GROUPS
 SLOTS = 7
+BACK_LAG = 3
+STORE_LAG = 4
 Z_PARTS = 2
 Z_GROUPS = GROUPS // Z_PARTS
 
@@ -43,13 +45,13 @@ def tile_scm_mlp_pa_kernel(tc, h_in, w, masks, mu, sigma, z, out):
         z_pool = ctx.enter_context(tc.tile_pool(name="z", bufs=LAYERS * Z_PARTS))
         w_pool = ctx.enter_context(tc.tile_pool(name="w", bufs=SLOTS))
         grouped_pool = ctx.enter_context(tc.tile_pool(name="grouped", bufs=2))
-        codes_pool = ctx.enter_context(tc.tile_pool(name="codes", bufs=3))
-        noise_pool = ctx.enter_context(tc.tile_pool(name="noise", bufs=5))
-        sums_pool = ctx.enter_context(tc.tile_pool(name="sums", bufs=3))
-        result_pool = ctx.enter_context(tc.tile_pool(name="result", bufs=3))
-        turned_psum = ctx.enter_context(tc.psum_pool(name="turned", bufs=2))
+        codes_pool = ctx.enter_context(tc.tile_pool(name="codes", bufs=4))
+        noise_pool = ctx.enter_context(tc.tile_pool(name="noise", bufs=4))
+        sums_pool = ctx.enter_context(tc.tile_pool(name="sums", bufs=2))
+        result_pool = ctx.enter_context(tc.tile_pool(name="result", bufs=4))
+        turned_psum = ctx.enter_context(tc.psum_pool(name="turned", bufs=3))
         z_psum = ctx.enter_context(tc.psum_pool(name="z_turned", bufs=1))
-        acc_psum = ctx.enter_context(tc.psum_pool(name="acc", bufs=3))
+        acc_psum = ctx.enter_context(tc.psum_pool(name="acc", bufs=2))
         back_psum = ctx.enter_context(tc.psum_pool(name="back", bufs=2))
 
         identity = keep.tile([P, P], F32)
@@ -235,6 +237,9 @@ def tile_scm_mlp_pa_kernel(tc, h_in, w, masks, mu, sigma, z, out):
                         identity=identity[:],
                     )
 
+        def by_vector(i, b):
+            return i >= STEPS - 2 and b == 1
+
         def finish(i, b):
             odd = i % 2
             if i >= STEPS - 2:
@@ -250,7 +255,7 @@ def tile_scm_mlp_pa_kernel(tc, h_in, w, masks, mu, sigma, z, out):
                 "q r (p e) -> q r p e", e=2
             )
             source = back[i, b][:].rearrange("q r e p -> q r p e")
-            if i >= STEPS - 2 and b == 1:
+            if by_vector(i, b):
                 nc.vector.tensor_scalar_max(out=target, in0=source, scalar1=0.0)
             else:
                 nc.scalar.activation(out=target, in_=source, func=FUNC.Relu)
@@ -262,7 +267,7 @@ def tile_scm_mlp_pa_kernel(tc, h_in, w, masks, mu, sigma, z, out):
                 out=out_view[:, tiles, GROUP * first : GROUP * (i + 1)], in_=result[i][:, tiles, :]
             )
 
-        z_behind = {1: 0, 4: 1, 6: 2, 8: 3}
+        z_behind = {1: 0, 4: 1, 7: 2, 10: 3}
 
         def load(i):
             if i < STEPS:
@@ -283,67 +288,64 @@ def tile_scm_mlp_pa_kernel(tc, h_in, w, masks, mu, sigma, z, out):
         make_table()
         mask_weights(0)
 
-        def turn_weights(i, passes):
-            if i < STEPS:
-                for g in passes:
-                    turn(i, w_sb[i], g)
+        def multiply_group(i):
+            if i == GROUPS:
+                order = [(0, 0), (0, 1), (1, 0), (1, 1), (0, 2), (1, 2)]
+            else:
+                order = [(e, g) for e in range(2) for g in range(PASSES)]
+            for e, g in order:
+                multiply(i, e, g)
 
-        def multiply_run(i, run):
-            if 0 <= i < STEPS:
-                if i == GROUPS:
-                    order = (((0, 0), (0, 1), (1, 0)), ((1, 1), (0, 2), (1, 2)))[run]
-                else:
-                    order = [(run, g) for g in range(PASSES)]
-                for e, g in order:
-                    multiply(i, e, g)
-
-        z_done = 0
-        for step in range(STEPS + 2):
-            z_end = min(STEPS, step + 1 + min(3, max(0, step - GROUPS + 2)))
-            z_now = range(z_done, z_end)
-            z_done = z_end
-            turn_weights(step, (0, 1))
-            multiply_run(step - 1, 0)
-            turn_weights(step, (2,))
-            for i in z_now[:1]:
-                turn_z(i)
-            if step == 0:
-                mask_weights(1)
-            if step < STEPS:
-                for g in range(PASSES):
-                    regroup(step, g)
-            for i in z_now[:1]:
-                make_noise(i)
-            multiply_run(step - 1, 1)
-            if step >= 2:
+        for step in range(STEPS + BACK_LAG + 1):
+            prepared = step if step < STEPS else None
+            multiplied = step - 1 if 1 <= step <= STEPS else None
+            finished = step - BACK_LAG if 0 <= step - BACK_LAG < STEPS else None
+            stored = step - STORE_LAG if 0 <= step - STORE_LAG < STEPS else None
+            if finished is not None:
                 for b in range(2):
-                    turn_back(step - 2, b)
-            if step < STEPS:
+                    turn_back(finished, b)
+            if prepared is not None:
                 for g in range(PASSES):
-                    quantise_weights(step, g)
+                    turn(prepared, w_sb[prepared], g)
+            if multiplied is not None:
+                multiply_group(multiplied)
+            if prepared is not None:
+                turn_z(prepared)
+            if finished is not None:
+                for b in range(2):
+                    if not by_vector(finished, b):
+                        finish(finished, b)
+            if prepared is not None:
+                for g in range(PASSES):
+                    regroup(prepared, g)
+                make_noise(prepared)
             late = step - 2 in (1, 3)
             if late:
                 round_a0((step - 2) // 2)
-            if 1 <= step <= STEPS:
-                for e in range(2):
-                    add_noise(step - 1, e)
+            if multiplied is not None:
+                add_noise(multiplied, 0)
+            if prepared is not None:
+                for g in range(PASSES):
+                    quantise_weights(prepared, g)
+            if multiplied is not None:
+                add_noise(multiplied, 1)
             if late:
                 quantise_a0((step - 2) // 2)
-            if step == GROUPS:
+            if multiplied == GROUPS - 1:
                 round_a0(PASSES - 1)
                 quantise_a0(PASSES - 1)
+            if step == 0:
+                mask_weights(1)
             if step + 2 < STEPS:
                 mask_weights(step + 2)
-            if step >= 2:
-                i = step - 2
+            if finished is not None:
                 for b in range(2):
-                    finish(i, b)
-                if i == STEPS - 2:
-                    store(i, range(2))
-                elif i >= STEPS - 2 or i % 2 == 1:
+                    if by_vector(finished, b):
+                        finish(finished, b)
+            if stored is not None:
+                if stored == STEPS - 2:
+                    store(stored, range(2))
+                elif stored == STEPS - 1 or stored % 2 == 1:
                     for b in range(2):
-                        store(i, range(b, b + 1))
-            for i in z_now[1:]:
-                turn_z(i)
-                make_noise(i)
+                        store(stored, range(b, b + 1))
             load(step + SLOTS - 1)

@@ -201,18 +201,23 @@ def tile_scm_mlp_pa_kernel(tc, h_in, w, masks, mu, sigma, z, out):
                     scale=table[:, 2 * (STEPS + i) + e : 2 * (STEPS + i) + e + 1],
                 )
 
-        def add_noise(i, e):
+        def add_noise(i, e, rows=slice(0, ROWS)):
             pair, odd = divmod(i, 2)
             if odd == 0 and e == 0:
                 sums[pair] = sums_pool.tile([P, 4, ROWS], F32, name="sums")
             nc.vector.tensor_tensor(
-                out=sums[pair][:, 2 * odd + e, :], in0=acc[i, e][:], in1=noise[i][:, e, :], op=ALU.add
+                out=sums[pair][:, 2 * odd + e, rows],
+                in0=acc[i, e][:, rows],
+                in1=noise[i][:, e, rows],
+                op=ALU.add,
             )
 
         def round_a0(pair):
             a_grouped[pair] = keep.tile([P, ROWS, 4], BF16, name="a_grouped", align_bytes=64)
             nc.vector.tensor_scalar_max(
-                out=a_grouped[pair][:], in0=sums[pair][:].rearrange("p t n -> p n t"), scalar1=0.0
+                out=a_grouped[pair][:].rearrange("p (c i) t -> p c t i", i=4),
+                in0=sums[pair][:].rearrange("p t (c i) -> p c t i", i=4),
+                scalar1=0.0,
             )
 
         def quantise_a0(pair):
@@ -222,20 +227,23 @@ def tile_scm_mlp_pa_kernel(tc, h_in, w, masks, mu, sigma, z, out):
                 in_=a_grouped[pair][:].rearrange("p n t -> p (n t)"),
             )
 
-        def turn_back(i, b):
+        def turn_back(i):
             pair, odd = divmod(i, 2)
+            places = [(b, r, e) for b in range(2) for r in range(2) for e in range(2)]
             if i == STEPS - 1:
-                back[i, b] = turned_psum.tile([P, 2, 2, P], F32, name="turned")
-            else:
-                back[i, b] = back_psum.tile([P, 2, 2, P], F32, name="back")
-            for r in range(2):
+                places = sorted(places, key=lambda place: place[2])
+            for b, r, e in places:
+                if (i, b) not in back:
+                    if i == STEPS - 1:
+                        back[i, b] = turned_psum.tile([P, 2, 2, P], F32, name="turned")
+                    else:
+                        back[i, b] = back_psum.tile([P, 2, 2, P], F32, name="back")
                 first_row = P * (2 * b + r)
-                for e in range(2):
-                    nc.tensor.transpose(
-                        out=back[i, b][:, r, e, :],
-                        in_=sums[pair][:, 2 * odd + e, first_row : first_row + P],
-                        identity=identity[:],
-                    )
+                nc.tensor.transpose(
+                    out=back[i, b][:, r, e, :],
+                    in_=sums[pair][:, 2 * odd + e, first_row : first_row + P],
+                    identity=identity[:],
+                )
 
         def by_vector(i, b):
             return i >= STEPS - 2 and b == 1
@@ -267,7 +275,7 @@ def tile_scm_mlp_pa_kernel(tc, h_in, w, masks, mu, sigma, z, out):
                 out=out_view[:, tiles, GROUP * first : GROUP * (i + 1)], in_=result[i][:, tiles, :]
             )
 
-        z_behind = {1: 0, 4: 1, 7: 2, 10: 3}
+        z_behind = {1: 0, 4: 1, 6: 2, 8: 3}
 
         def load(i):
             if i < STEPS:
@@ -296,29 +304,36 @@ def tile_scm_mlp_pa_kernel(tc, h_in, w, masks, mu, sigma, z, out):
             for e, g in order:
                 multiply(i, e, g)
 
+        z_done = 0
         for step in range(STEPS + BACK_LAG + 1):
             prepared = step if step < STEPS else None
             multiplied = step - 1 if 1 <= step <= STEPS else None
             finished = step - BACK_LAG if 0 <= step - BACK_LAG < STEPS else None
             stored = step - STORE_LAG if 0 <= step - STORE_LAG < STEPS else None
+            z_end = min(STEPS, step + 1 + min(2, max(0, step - GROUPS + 1)))
+            z_now = list(range(z_done, z_end))
+            z_done = z_end
             if finished is not None:
-                for b in range(2):
-                    turn_back(finished, b)
+                turn_back(finished)
             if prepared is not None:
                 for g in range(PASSES):
                     turn(prepared, w_sb[prepared], g)
+            for i in z_now[:-1]:
+                turn_z(i)
             if multiplied is not None:
                 multiply_group(multiplied)
-            if prepared is not None:
-                turn_z(prepared)
             if finished is not None:
                 for b in range(2):
                     if not by_vector(finished, b):
                         finish(finished, b)
+            for i in z_now[:-1]:
+                make_noise(i)
             if prepared is not None:
                 for g in range(PASSES):
                     regroup(prepared, g)
-                make_noise(prepared)
+            for i in z_now[-1:]:
+                turn_z(i)
+                make_noise(i)
             late = step - 2 in (1, 3)
             if late:
                 round_a0((step - 2) // 2)
@@ -327,7 +342,10 @@ def tile_scm_mlp_pa_kernel(tc, h_in, w, masks, mu, sigma, z, out):
             if prepared is not None:
                 for g in range(PASSES):
                     quantise_weights(prepared, g)
-            if multiplied is not None:
+            if multiplied == STEPS - 1:
+                for b in range(2):
+                    add_noise(multiplied, 1, slice(2 * P * b, 2 * P * (b + 1)))
+            elif multiplied is not None:
                 add_noise(multiplied, 1)
             if late:
                 quantise_a0((step - 2) // 2)

@@ -46,7 +46,7 @@ def tile_scm_mlp_pa_kernel(tc, h_in, w, masks, mu, sigma, z, out):
         w_pool = ctx.enter_context(tc.tile_pool(name="w", bufs=SLOTS))
         grouped_pool = ctx.enter_context(tc.tile_pool(name="grouped", bufs=2))
         codes_pool = ctx.enter_context(tc.tile_pool(name="codes", bufs=4))
-        noise_pool = ctx.enter_context(tc.tile_pool(name="noise", bufs=4))
+        noise_pool = ctx.enter_context(tc.tile_pool(name="noise", bufs=6))
         sums_pool = ctx.enter_context(tc.tile_pool(name="sums", bufs=2))
         result_pool = ctx.enter_context(tc.tile_pool(name="result", bufs=4))
         turned_psum = ctx.enter_context(tc.psum_pool(name="turned", bufs=3))
@@ -310,30 +310,32 @@ def tile_scm_mlp_pa_kernel(tc, h_in, w, masks, mu, sigma, z, out):
             multiplied = step - 1 if 1 <= step <= STEPS else None
             finished = step - BACK_LAG if 0 <= step - BACK_LAG < STEPS else None
             stored = step - STORE_LAG if 0 <= step - STORE_LAG < STEPS else None
-            z_end = min(STEPS, step + 1 + min(2, max(0, step - GROUPS + 1)))
+            z_end = min(STEPS, step + min(3, max(0, step - GROUPS + 2)))
             z_now = list(range(z_done, z_end))
             z_done = z_end
+            for i in z_now[:1]:
+                turn_z(i)
             if finished is not None:
                 turn_back(finished)
             if prepared is not None:
                 for g in range(PASSES):
                     turn(prepared, w_sb[prepared], g)
-            for i in z_now[:-1]:
+            for i in z_now[1:]:
+                make_noise(i - 1)
                 turn_z(i)
             if multiplied is not None:
                 multiply_group(multiplied)
+            if len(z_now) == 1:
+                make_noise(z_now[0])
             if finished is not None:
                 for b in range(2):
                     if not by_vector(finished, b):
                         finish(finished, b)
-            for i in z_now[:-1]:
+            for i in z_now[1:]:
                 make_noise(i)
             if prepared is not None:
                 for g in range(PASSES):
                     regroup(prepared, g)
-            for i in z_now[-1:]:
-                turn_z(i)
-                make_noise(i)
             late = step - 2 in (1, 3)
             if late:
                 round_a0((step - 2) // 2)
@@ -361,9 +363,7 @@ def tile_scm_mlp_pa_kernel(tc, h_in, w, masks, mu, sigma, z, out):
                     if by_vector(finished, b):
                         finish(finished, b)
             if stored is not None:
-                if stored == STEPS - 2:
-                    store(stored, range(2))
-                elif stored == STEPS - 1 or stored % 2 == 1:
+                if stored >= STEPS - 2 or stored % 2 == 1:
                     for b in range(2):
                         store(stored, range(b, b + 1))
             load(step + SLOTS - 1)

@@ -21,9 +21,8 @@ PASSES = FEATURES // K_PASS
 GROUP = 2 * P
 GROUPS = FEATURES // GROUP
 STEPS = LAYERS * GROUPS
-SLOTS = 7
+SLOTS = 6
 BACK_LAG = 3
-STORE_LAG = 4
 Z_PARTS = 2
 Z_GROUPS = GROUPS // Z_PARTS
 
@@ -48,7 +47,7 @@ def tile_scm_mlp_pa_kernel(tc, h_in, w, masks, mu, sigma, z, out):
         codes_pool = ctx.enter_context(tc.tile_pool(name="codes", bufs=4))
         noise_pool = ctx.enter_context(tc.tile_pool(name="noise", bufs=6))
         sums_pool = ctx.enter_context(tc.tile_pool(name="sums", bufs=2))
-        result_pool = ctx.enter_context(tc.tile_pool(name="result", bufs=4))
+        result_pool = ctx.enter_context(tc.tile_pool(name="result", bufs=2))
         turned_psum = ctx.enter_context(tc.psum_pool(name="turned", bufs=3))
         z_psum = ctx.enter_context(tc.psum_pool(name="z_turned", bufs=1))
         acc_psum = ctx.enter_context(tc.psum_pool(name="acc", bufs=2))
@@ -227,55 +226,73 @@ def tile_scm_mlp_pa_kernel(tc, h_in, w, masks, mu, sigma, z, out):
                 in_=a_grouped[pair][:].rearrange("p n t -> p (n t)"),
             )
 
+        def pieces(i):
+            count = ROW_TILES if i == STEPS - 1 else 2
+            return [slice(n * ROW_TILES // count, (n + 1) * ROW_TILES // count) for n in range(count)]
+
         def turn_back(i):
             pair, odd = divmod(i, 2)
-            places = [(b, r, e) for b in range(2) for r in range(2) for e in range(2)]
+            back[i] = []
+            for n, tiles in enumerate(pieces(i)):
+                shape = [P, tiles.stop - tiles.start, 2, P]
+                if i == STEPS - 1 and n < PASSES:
+                    back[i].append(turned_psum.tile(shape, F32, name="turned"))
+                else:
+                    back[i].append(back_psum.tile(shape, F32, name="back"))
+            places = [(n, e) for n in range(len(back[i])) for e in range(2)]
             if i == STEPS - 1:
-                places = sorted(places, key=lambda place: place[2])
-            for b, r, e in places:
-                if (i, b) not in back:
-                    if i == STEPS - 1:
-                        back[i, b] = turned_psum.tile([P, 2, 2, P], F32, name="turned")
-                    else:
-                        back[i, b] = back_psum.tile([P, 2, 2, P], F32, name="back")
-                first_row = P * (2 * b + r)
-                nc.tensor.transpose(
-                    out=back[i, b][:, r, e, :],
-                    in_=sums[pair][:, 2 * odd + e, first_row : first_row + P],
-                    identity=identity[:],
-                )
+                places = sorted(places, key=lambda place: 2 * (place[0] == PASSES) + place[1])
+            for n, e in places:
+                tiles = pieces(i)[n]
+                for r in range(tiles.start, tiles.stop):
+                    nc.tensor.transpose(
+                        out=back[i][n][:, r - tiles.start, e, :],
+                        in_=sums[pair][:, 2 * odd + e, P * r : P * (r + 1)],
+                        identity=identity[:],
+                    )
 
-        def by_vector(i, b):
-            return i >= STEPS - 2 and b == 1
+        def by_vector(i, n):
+            return i >= STEPS - 2 and 2 * n >= len(pieces(i))
 
-        def finish(i, b):
+        def finish(i, n):
             odd = i % 2
-            if i >= STEPS - 2:
-                if b == 0:
-                    result[i] = result_pool.tile([P, ROW_TILES, GROUP], F32, name="result")
-                columns = slice(0, GROUP)
+            if n == 0 and i == 0:
+                result[i] = keep.tile([P, ROW_TILES, FEATURES], F32, name="layer_result")
+            elif n == 0 and i == STEPS - 2:
+                result[i] = keep.tile([P, 2, ROW_TILES, GROUP], F32, name="layer_result")
+            elif n == 0 and i >= GROUPS and odd == 0:
+                result[i] = result_pool.tile([P, ROW_TILES, 2 * GROUP], F32, name="pair_result")
+            elif n == 0:
+                result[i] = result[i - 1]
+            if i < GROUPS:
+                block = result[i][:, :, GROUP * i : GROUP * (i + 1)]
+            elif i < STEPS - 2:
+                block = result[i][:, :, GROUP * odd : GROUP * (odd + 1)]
             else:
-                if odd == 0 and b == 0:
-                    result[i] = result_pool.tile([P, ROW_TILES, 2 * GROUP], F32, name="result")
-                    result[i + 1] = result[i]
-                columns = slice(GROUP * odd, GROUP * (odd + 1))
-            target = result[i][:, 2 * b : 2 * b + 2, columns].rearrange(
-                "q r (p e) -> q r p e", e=2
-            )
-            source = back[i, b][:].rearrange("q r e p -> q r p e")
-            if by_vector(i, b):
+                block = result[i][:, odd, :, :]
+            target = block[:, pieces(i)[n], :].rearrange("q r (p e) -> q r p e", e=2)
+            source = back[i][n][:].rearrange("q r e p -> q r p e")
+            if by_vector(i, n):
                 nc.vector.tensor_scalar_max(out=target, in0=source, scalar1=0.0)
             else:
                 nc.scalar.activation(out=target, in_=source, func=FUNC.Relu)
 
-        def store(i, halves):
-            first = i if i >= STEPS - 2 else i - 1
-            tiles = slice(2 * halves[0], 2 * halves[-1] + 2)
-            nc.sync.dma_start(
-                out=out_view[:, tiles, GROUP * first : GROUP * (i + 1)], in_=result[i][:, tiles, :]
-            )
+        def store(i):
+            if i == GROUPS - 1:
+                for r in range(ROW_TILES):
+                    nc.sync.dma_start(out=out_view[:, r, 0:FEATURES], in_=result[i][:, r, :])
+            elif i >= STEPS - 2 or (i > GROUPS and i % 2 == 1):
+                first = i if i >= STEPS - 2 else i - 1
+                for tiles in pieces(i):
+                    if i >= STEPS - 2:
+                        source = result[i][:, i % 2, tiles, :]
+                    else:
+                        source = result[i][:, tiles, :]
+                    nc.sync.dma_start(
+                        out=out_view[:, tiles, GROUP * first : GROUP * (i + 1)], in_=source
+                    )
 
-        z_behind = {1: 0, 4: 1, 6: 2, 8: 3}
+        z_behind = {1: 0, 4: 1, 6: 2, 7: 3}
 
         def load(i):
             if i < STEPS:
@@ -305,11 +322,10 @@ def tile_scm_mlp_pa_kernel(tc, h_in, w, masks, mu, sigma, z, out):
                 multiply(i, e, g)
 
         z_done = 0
-        for step in range(STEPS + BACK_LAG + 1):
+        for step in range(STEPS + BACK_LAG):
             prepared = step if step < STEPS else None
             multiplied = step - 1 if 1 <= step <= STEPS else None
             finished = step - BACK_LAG if 0 <= step - BACK_LAG < STEPS else None
-            stored = step - STORE_LAG if 0 <= step - STORE_LAG < STEPS else None
             z_end = min(STEPS, step + min(3, max(0, step - GROUPS + 2)))
             z_now = list(range(z_done, z_end))
             z_done = z_end
@@ -328,9 +344,9 @@ def tile_scm_mlp_pa_kernel(tc, h_in, w, masks, mu, sigma, z, out):
             if len(z_now) == 1:
                 make_noise(z_now[0])
             if finished is not None:
-                for b in range(2):
-                    if not by_vector(finished, b):
-                        finish(finished, b)
+                for n in range(len(pieces(finished))):
+                    if not by_vector(finished, n):
+                        finish(finished, n)
             for i in z_now[1:]:
                 make_noise(i)
             if prepared is not None:
@@ -345,8 +361,8 @@ def tile_scm_mlp_pa_kernel(tc, h_in, w, masks, mu, sigma, z, out):
                 for g in range(PASSES):
                     quantise_weights(prepared, g)
             if multiplied == STEPS - 1:
-                for b in range(2):
-                    add_noise(multiplied, 1, slice(2 * P * b, 2 * P * (b + 1)))
+                for tiles in pieces(multiplied):
+                    add_noise(multiplied, 1, slice(P * tiles.start, P * tiles.stop))
             elif multiplied is not None:
                 add_noise(multiplied, 1)
             if late:
@@ -359,11 +375,9 @@ def tile_scm_mlp_pa_kernel(tc, h_in, w, masks, mu, sigma, z, out):
             if step + 2 < STEPS:
                 mask_weights(step + 2)
             if finished is not None:
-                for b in range(2):
-                    if by_vector(finished, b):
-                        finish(finished, b)
-            if stored is not None:
-                if stored >= STEPS - 2 or stored % 2 == 1:
-                    for b in range(2):
-                        store(stored, range(b, b + 1))
+                for n in range(len(pieces(finished))):
+                    if by_vector(finished, n):
+                        finish(finished, n)
+            if finished is not None:
+                store(finished)
             load(step + SLOTS - 1)

@@ -211,19 +211,20 @@ def tile_scm_mlp_pa_kernel(tc, h_in, w, masks, mu, sigma, z, out):
                 op=ALU.add,
             )
 
-        def round_a0(pair):
-            a_grouped[pair] = keep.tile([P, ROWS, 4], BF16, name="a_grouped", align_bytes=64)
+        def round_a0(pair, rows=slice(0, ROWS)):
+            if rows.start == 0:
+                a_grouped[pair] = keep.tile([P, ROWS, 4], BF16, name="a_grouped", align_bytes=64)
             nc.vector.tensor_scalar_max(
-                out=a_grouped[pair][:].rearrange("p (c i) t -> p c t i", i=4),
-                in0=sums[pair][:].rearrange("p t (c i) -> p c t i", i=4),
+                out=a_grouped[pair][:, rows, :].rearrange("p (c i) t -> p c t i", i=4),
+                in0=sums[pair][:, :, rows].rearrange("p t (c i) -> p c t i", i=4),
                 scalar1=0.0,
             )
 
-        def quantise_a0(pair):
+        def quantise_a0(pair, rows=slice(0, ROWS)):
             nc.vector.quantize_mx(
-                out=act_codes[1][:, pair, :].bitcast(FP8X4),
-                scales=act_scales[1][:, pair, :],
-                in_=a_grouped[pair][:].rearrange("p n t -> p (n t)"),
+                out=act_codes[1][:, pair, rows].bitcast(FP8X4),
+                scales=act_scales[1][:, pair, rows],
+                in_=a_grouped[pair][:, rows, :].rearrange("p n t -> p (n t)"),
             )
 
         def pieces(i):
@@ -341,7 +342,7 @@ def tile_scm_mlp_pa_kernel(tc, h_in, w, masks, mu, sigma, z, out):
                 turn_z(i)
             if multiplied is not None:
                 multiply_group(multiplied)
-            if len(z_now) == 1:
+            if len(z_now) == 1 and step > 1:
                 make_noise(z_now[0])
             if finished is not None:
                 for n in range(len(pieces(finished))):
@@ -352,27 +353,37 @@ def tile_scm_mlp_pa_kernel(tc, h_in, w, masks, mu, sigma, z, out):
             if prepared is not None:
                 for g in range(PASSES):
                     regroup(prepared, g)
+            if step == 1:
+                make_noise(0)
             late = step - 2 in (1, 3)
             if late:
                 round_a0((step - 2) // 2)
-            if multiplied is not None:
+            if step == 0:
+                mask_weights(1)
+            if multiplied is not None and step > 1:
                 add_noise(multiplied, 0)
             if prepared is not None:
-                for g in range(PASSES):
+                for g in range(PASSES - 1):
                     quantise_weights(prepared, g)
+                if multiplied == GROUPS - 1:
+                    add_noise(multiplied, 1)
+                quantise_weights(prepared, PASSES - 1)
+            if step == 1:
+                mask_weights(2)
+                add_noise(multiplied, 0)
             if multiplied == STEPS - 1:
                 for tiles in pieces(multiplied):
                     add_noise(multiplied, 1, slice(P * tiles.start, P * tiles.stop))
-            elif multiplied is not None:
+            elif multiplied is not None and multiplied != GROUPS - 1:
                 add_noise(multiplied, 1)
             if late:
                 quantise_a0((step - 2) // 2)
             if multiplied == GROUPS - 1:
-                round_a0(PASSES - 1)
-                quantise_a0(PASSES - 1)
-            if step == 0:
-                mask_weights(1)
-            if step + 2 < STEPS:
+                for half in range(2):
+                    round_a0(PASSES - 1, slice(ROWS // 2 * half, ROWS // 2 * (half + 1)))
+                for half in range(2):
+                    quantise_a0(PASSES - 1, slice(ROWS // 2 * half, ROWS // 2 * (half + 1)))
+            if 0 < step < STEPS - 2:
                 mask_weights(step + 2)
             if finished is not None:
                 for n in range(len(pieces(finished))):

@@ -106,10 +106,10 @@ def tile_scm_mlp_pa_kernel(tc, h_in, w, masks, mu, sigma, z, out):
         act_scales = []
         for layer in range(LAYERS):
             act_codes.append(
-                keep.tile([P, PASSES, ROWS], U32, name="act_codes%d" % layer, align_bytes=64)
+                keep.tile([P, PASSES, ROWS], U32, name="act_codes%d" % layer, align_bytes=256)
             )
             act_scales.append(
-                keep.tile([P, PASSES, ROWS], U8, name="act_scales%d" % layer, align_bytes=64)
+                keep.tile([P, PASSES, ROWS], U8, name="act_scales%d" % layer, align_bytes=256)
             )
         table = keep.tile([P, 4 * STEPS], F32)
 
@@ -142,8 +142,8 @@ def tile_scm_mlp_pa_kernel(tc, h_in, w, masks, mu, sigma, z, out):
 
         def quantise_weights(i, g):
             if g == 0:
-                codes[i] = codes_pool.tile([P, PASSES, GROUP], U32, name="codes", align_bytes=64)
-                scales[i] = codes_pool.tile([P, PASSES, GROUP], U8, name="scales", align_bytes=64)
+                codes[i] = codes_pool.tile([P, PASSES, GROUP], U32, name="codes", align_bytes=256)
+                scales[i] = codes_pool.tile([P, PASSES, GROUP], U8, name="scales", align_bytes=256)
             nc.vector.quantize_mx(
                 out=codes[i][:, g, :].bitcast(FP8X4),
                 scales=scales[i][:, g, :],
@@ -165,7 +165,9 @@ def tile_scm_mlp_pa_kernel(tc, h_in, w, masks, mu, sigma, z, out):
 
         def multiply(i, e, g):
             layer = i // GROUPS
-            if g == 0:
+            if g == 0 and (2 * i + e) % 3 == 2 and i >= STEPS - 3:
+                acc[i, e] = z_psum.tile([P, ROWS], F32, name="z_bank")
+            elif g == 0:
                 acc[i, e] = acc_psum.tile([P, ROWS], F32, name="acc")
             tile_columns = slice(P * e, P * (e + 1))
             nc.tensor.matmul_mx(

from contextlib import ExitStack

import concourse.masks as masks_lib
import concourse.mybir as mybir

F32 = mybir.dt.float32
BF16 = mybir.dt.bfloat16
U32 = mybir.dt.uint32
U8 = mybir.dt.uint8
FP8X4 = mybir.dt.float8_e4m3fn_x4
FUNC = mybir.ActivationFunctionType
ALU = mybir.AluOpType

P = 128
LAYERS = 2
ROWS = 512
ROW_TILES = ROWS // P
FEATURES = 1536
K_PASS = 4 * P
PASSES = FEATURES // K_PASS
GROUP = 2 * P
GROUPS = FEATURES // GROUP
STEPS = LAYERS * GROUPS
SLOTS = 6
BACK_LAG = 3
Z_PARTS = 2
Z_GROUPS = GROUPS // Z_PARTS

FLOPS = 2 * LAYERS * ROWS * FEATURES * FEATURES


def tile_scm_mlp_pa_kernel(tc, h_in, w, masks, mu, sigma, z, out):
    nc = tc.nc

    h_view = h_in.rearrange("(q r) k -> q r k", q=P)
    w_view = w.rearrange("l (u p e) k -> l u p e k", p=P, e=2)
    m_view = masks.rearrange("l (u p e) k -> l u p e k", p=P, e=2)
    z_view = z.rearrange("l (q r) f -> l q r f", q=P)
    out_view = out.rearrange("(q r) f -> q r f", q=P)

    with ExitStack() as ctx:
        ctx.enter_context(tc.manual_schedule())
        keep = ctx.enter_context(tc.tile_pool(name="keep", bufs=1))
        z_pool = ctx.enter_context(tc.tile_pool(name="z", bufs=LAYERS * Z_PARTS))
        w_pool = ctx.enter_context(tc.tile_pool(name="w", bufs=SLOTS))
        grouped_pool = ctx.enter_context(tc.tile_pool(name="grouped", bufs=2))
        codes_pool = ctx.enter_context(tc.tile_pool(name="codes", bufs=4))
        noise_pool = ctx.enter_context(tc.tile_pool(name="noise", bufs=6))
        sums_pool = ctx.enter_context(tc.tile_pool(name="sums", bufs=2))
        result_pool = ctx.enter_context(tc.tile_pool(name="result", bufs=2))
        turned_psum = ctx.enter_context(tc.psum_pool(name="turned", bufs=3))
        z_psum = ctx.enter_context(tc.psum_pool(name="z_turned", bufs=1))
        acc_psum = ctx.enter_context(tc.psum_pool(name="acc", bufs=2))
        back_psum = ctx.enter_context(tc.psum_pool(name="back", bufs=2))

        identity = keep.tile([P, P], F32)
        masks_lib.make_identity(nc, identity[:])

        rows = keep.tile([P, GROUP], BF16)
        nc.vector.memset(rows[:], 0.0)

        w_sb = {}
        m_sb = {}
        z_sb = {}
        h_sb = {}

        def load_weights(i, halves=False):
            layer, u = divmod(i, GROUPS)
            w_sb[i] = w_pool.tile([P, 2, FEATURES], BF16, name="w_sb")
            m_sb[i] = w_pool.tile([P, 2, FEATURES], BF16, name="m_sb")
            parts = [slice(0, 1), slice(1, 2)] if halves else [slice(0, 2)]
            for part in parts:
                nc.sync.dma_start(out=w_sb[i][:, part, :], in_=w_view[layer, u][:, part, :])
                nc.sync.dma_start(out=m_sb[i][:, part, :], in_=m_view[layer, u][:, part, :])

        def load_h():
            h_sb[0] = w_pool.tile([P, 2, FEATURES], BF16, name="w_sb")
            h_sb[1] = w_pool.tile([P, 2, FEATURES], BF16, name="m_sb")
            for b in range(2):
                nc.sync.dma_start(out=h_sb[b][:], in_=h_view[:, 2 * b : 2 * b + 2, :])
            nc.sync.dma_start(out=rows[0:STEPS, :], in_=mu.rearrange("l (u f) -> (l u) f", f=GROUP))
            nc.sync.dma_start(
                out=rows[STEPS : 2 * STEPS, :], in_=sigma.rearrange("l (u f) -> (l u) f", f=GROUP)
            )

        def load_z(part):
            layer, half = divmod(part, Z_PARTS)
            columns = GROUP * Z_GROUPS
            z_sb[part] = z_pool.tile([P, ROW_TILES, columns], BF16, name="z_sb")
            nc.sync.dma_start(
                out=z_sb[part][:], in_=z_view[layer][:, :, columns * half : columns * (half + 1)]
            )

        turned = {}
        grouped = {}
        codes = {}
        scales = {}
        z_bank = {}
        noise = {}
        acc = {}
        sums = {}
        a_grouped = {}
        back = {}
        result = {}
        act_codes = []
        act_scales = []
        for layer in range(LAYERS):
            act_codes.append(
                keep.tile([P, PASSES, ROWS], U32, name="act_codes%d" % layer, align_bytes=256)
            )
            act_scales.append(
                keep.tile([P, PASSES, ROWS], U8, name="act_scales%d" % layer, align_bytes=256)
            )
        table = keep.tile([P, 4 * STEPS], F32)

        def mask_weights(i, part=slice(0, 2)):
            nc.vector.tensor_tensor(
                out=w_sb[i][:, part, :], in0=w_sb[i][:, part, :], in1=m_sb[i][:, part, :], op=ALU.mult
            )

        def turn(key, block, g):
            bank = turned_psum.tile([P, 2, 2, P], F32, name="turned")
            for half in range(2):
                first_word = (K_PASS // 2) * g + P * half
                for e in range(2):
                    nc.tensor.transpose(
                        out=bank[:, half, e, :],
                        in_=block[:, e, :].bitcast(F32)[:, first_word : first_word + P],
                        identity=identity[:],
                    )
            turned[key, g] = bank

        def regroup(key, g):
            if g == 0:
                grouped[key] = grouped_pool.tile(
                    [P, PASSES, 4 * GROUP], BF16, name="grouped", align_bytes=64
                )
            nc.scalar.copy(
                out=grouped[key][:, g, :].bitcast(F32).rearrange("p (c half) -> p c half", half=2),
                in_=turned[key, g][:].rearrange("p half e c -> p (e c) half"),
            )

        def quantise_weights(i, g):
            if g == 0:
                codes[i] = codes_pool.tile([P, PASSES, GROUP], U32, name="codes", align_bytes=256)
                scales[i] = codes_pool.tile([P, PASSES, GROUP], U8, name="scales", align_bytes=256)
            nc.vector.quantize_mx(
                out=codes[i][:, g, :].bitcast(FP8X4),
                scales=scales[i][:, g, :],
                in_=grouped[i][:, g, :],
            )

        def quantise_h(b, g):
            columns = slice(2 * P * b, 2 * P * (b + 1))
            nc.vector.quantize_mx(
                out=act_codes[0][:, g, columns].bitcast(FP8X4),
                scales=act_scales[0][:, g, columns],
                in_=grouped["h", b][:, g, :],
            )

        def make_table():
            bank = z_psum.tile([P, ROWS], F32, name="z_bank")
            nc.tensor.transpose(out=bank[:, 0:P], in_=rows[:].bitcast(F32), identity=identity[:])
            nc.vector.tensor_copy(out=table[:], in_=bank[:, 0 : 2 * STEPS].bitcast(BF16))

        def multiply(i, e, g):
            layer = i // GROUPS
            if g == 0 and (2 * i + e) % 3 == 2 and i >= STEPS - 3:
                acc[i, e] = z_psum.tile([P, ROWS], F32, name="z_bank")
            elif g == 0:
                acc[i, e] = acc_psum.tile([P, ROWS], F32, name="acc")
            tile_columns = slice(P * e, P * (e + 1))
            nc.tensor.matmul_mx(
                out=acc[i, e][:],
                lhsT=codes[i][:, g, tile_columns].bitcast(FP8X4),
                lhsT_scale=scales[i][:, g, tile_columns],
                rhs=act_codes[layer][:, g, :].bitcast(FP8X4),
                rhs_scale=act_scales[layer][:, g, :],
                start=(g == 0),
                stop=(g == PASSES - 1),
            )

        def turn_z(i):
            part, place = divmod(i, Z_GROUPS)
            z_bank[i] = z_psum.tile([P, ROWS], F32, name="z_bank")
            for r in range(ROW_TILES):
                nc.tensor.transpose(
                    out=z_bank[i][:, P * r : P * (r + 1)],
                    in_=z_sb[part][:, r, :].bitcast(F32)[:, P * place : P * (place + 1)],
                    identity=identity[:],
                )

        def make_noise(i):
            noise[i] = noise_pool.tile([P, 2, ROWS], F32, name="noise")
            z_pairs = z_bank[i][:].bitcast(BF16).rearrange("p (n e) -> p n e", e=2)
            for e in range(2):
                nc.scalar.activation(
                    out=noise[i][:, e, :],
                    in_=z_pairs[:, :, e],
                    func=FUNC.Exp,
                    bias=table[:, 2 * i + e : 2 * i + e + 1],
                    scale=table[:, 2 * (STEPS + i) + e : 2 * (STEPS + i) + e + 1],
                )

        def add_noise(i, e, rows=slice(0, ROWS)):
            pair, odd = divmod(i, 2)
            if odd == 0 and e == 0:
                sums[pair] = sums_pool.tile([P, 4, ROWS], F32, name="sums")
            nc.vector.tensor_tensor(
                out=sums[pair][:, 2 * odd + e, rows],
                in0=acc[i, e][:, rows],
                in1=noise[i][:, e, rows],
                op=ALU.add,
            )

        def round_a0(pair, rows=slice(0, ROWS)):
            if rows.start == 0:
                a_grouped[pair] = keep.tile([P, ROWS, 4], BF16, name="a_grouped", align_bytes=64)
            nc.vector.tensor_scalar_max(
                out=a_grouped[pair][:, rows, :].rearrange("p (c i) t -> p c t i", i=4),
                in0=sums[pair][:, :, rows].rearrange("p t (c i) -> p c t i", i=4),
                scalar1=0.0,
            )

        def quantise_a0(pair, rows=slice(0, ROWS)):
            nc.vector.quantize_mx(
                out=act_codes[1][:, pair, rows].bitcast(FP8X4),
                scales=act_scales[1][:, pair, rows],
                in_=a_grouped[pair][:, rows, :].rearrange("p n t -> p (n t)"),
            )

        def pieces(i):
            count = ROW_TILES if i == STEPS - 1 else 2
            return [slice(n * ROW_TILES // count, (n + 1) * ROW_TILES // count) for n in range(count)]

        def turn_back(i):
            pair, odd = divmod(i, 2)
            back[i] = []
            for n, tiles in enumerate(pieces(i)):
                shape = [P, tiles.stop - tiles.start, 2, P]
                if i == STEPS - 1 and n < PASSES:
                    back[i].append(turned_psum.tile(shape, F32, name="turned"))
                else:
                    back[i].append(back_psum.tile(shape, F32, name="back"))
            places = [(n, e) for n in range(len(back[i])) for e in range(2)]
            if i == STEPS - 1:
                places = sorted(places, key=lambda place: 2 * (place[0] == PASSES) + place[1])
            for n, e in places:
                tiles = pieces(i)[n]
                for r in range(tiles.start, tiles.stop):
                    nc.tensor.transpose(
                        out=back[i][n][:, r - tiles.start, e, :],
                        in_=sums[pair][:, 2 * odd + e, P * r : P * (r + 1)],
                        identity=identity[:],
                    )

        def by_vector(i, n):
            return i >= STEPS - 2 and 2 * n >= len(pieces(i))

        def finish(i, n):
            odd = i % 2
            if n == 0 and i == 0:
                result[i] = keep.tile([P, ROW_TILES, FEATURES], F32, name="layer_result")
            elif n == 0 and i == STEPS - 2:
                result[i] = keep.tile([P, 2, ROW_TILES, GROUP], F32, name="layer_result")
            elif n == 0 and i >= GROUPS and odd == 0:
                result[i] = result_pool.tile([P, ROW_TILES, 2 * GROUP], F32, name="pair_result")
            elif n == 0:
                result[i] = result[i - 1]
            if i < GROUPS:
                block = result[i][:, :, GROUP * i : GROUP * (i + 1)]
            elif i < STEPS - 2:
                block = result[i][:, :, GROUP * odd : GROUP * (odd + 1)]
            else:
                block = result[i][:, odd, :, :]
            target = block[:, pieces(i)[n], :].rearrange("q r (p e) -> q r p e", e=2)
            source = back[i][n][:].rearrange("q r e p -> q r p e")
            if by_vector(i, n):
                nc.vector.tensor_scalar_max(out=target, in0=source, scalar1=0.0)
            else:
                nc.scalar.activation(out=target, in_=source, func=FUNC.Relu)

        def store(i):
            if i == GROUPS - 1:
                for r in range(ROW_TILES):
                    nc.sync.dma_start(out=out_view[:, r, 0:FEATURES], in_=result[i][:, r, :])
            elif i >= STEPS - 2 or (i > GROUPS and i % 2 == 1):
                first = i if i >= STEPS - 2 else i - 1
                for tiles in pieces(i):
                    if i >= STEPS - 2:
                        source = result[i][:, i % 2, tiles, :]
                    else:
                        source = result[i][:, tiles, :]
                    nc.sync.dma_start(
                        out=out_view[:, tiles, GROUP * first : GROUP * (i + 1)], in_=source
                    )

        z_behind = {1: 0, 4: 1, 6: 2, 7: 3}

        def load(i):
            if i < STEPS:
                load_weights(i)
                if i in z_behind:
                    load_z(z_behind[i])

        load_h()
        for i in range(SLOTS - 1):
            load(i)

        for b in range(2):
            for g in range(PASSES):
                turn(("h", b), h_sb[b], g)
                regroup(("h", b), g)
            for g in range(PASSES):
                quantise_h(b, g)
        make_table()
        mask_weights(0)

        def multiply_group(i):
            if i == GROUPS:
                order = [(0, 0), (0, 1), (1, 0), (1, 1), (0, 2), (1, 2)]
            else:
                order = [(e, g) for e in range(2) for g in range(PASSES)]
            for e, g in order:
                multiply(i, e, g)

        z_done = 0
        for step in range(STEPS + BACK_LAG):
            prepared = step if step < STEPS else None
            multiplied = step - 1 if 1 <= step <= STEPS else None
            finished = step - BACK_LAG if 0 <= step - BACK_LAG < STEPS else None
            z_end = min(STEPS, step + min(3, max(0, step - GROUPS + 2)))
            z_now = list(range(z_done, z_end))
            z_done = z_end
            for i in z_now[:1]:
                turn_z(i)
            if finished is not None:
                turn_back(finished)
            if prepared is not None:
                for g in range(PASSES):
                    turn(prepared, w_sb[prepared], g)
            for i in z_now[1:]:
                make_noise(i - 1)
                turn_z(i)
            if multiplied is not None:
                multiply_group(multiplied)
            if len(z_now) == 1 and step > 1:
                make_noise(z_now[0])
            if finished is not None:
                for n in range(len(pieces(finished))):
                    if not by_vector(finished, n):
                        finish(finished, n)
            for i in z_now[1:]:
                make_noise(i)
            if prepared is not None:
                for g in range(PASSES):
                    regroup(prepared, g)
            if step == 1:
                make_noise(0)
            late = step - 2 in (1, 3)
            if late:
                round_a0((step - 2) // 2)
            if step == 0:
                mask_weights(1)
            if multiplied is not None and step > 1:
                add_noise(multiplied, 0)
            if prepared is not None:
                for g in range(PASSES - 1):
                    quantise_weights(prepared, g)
                if multiplied == GROUPS - 1:
                    add_noise(multiplied, 1)
                quantise_weights(prepared, PASSES - 1)
            if step == 1:
                mask_weights(2)
                add_noise(multiplied, 0)
            if multiplied == STEPS - 1:
                for tiles in pieces(multiplied):
                    add_noise(multiplied, 1, slice(P * tiles.start, P * tiles.stop))
            elif multiplied is not None and multiplied != GROUPS - 1:
                add_noise(multiplied, 1)
            if late:
                quantise_a0((step - 2) // 2)
            if multiplied == GROUPS - 1:
                for half in range(2):
                    round_a0(PASSES - 1, slice(ROWS // 2 * half, ROWS // 2 * (half + 1)))
                for half in range(2):
                    quantise_a0(PASSES - 1, slice(ROWS // 2 * half, ROWS // 2 * (half + 1)))
            if 0 < step < STEPS - 2:
                mask_weights(step + 2)
            if finished is not None:
                for n in range(len(pieces(finished))):
                    if by_vector(finished, n):
                        finish(finished, n)
            if finished is not None:
                store(finished)
            load(step + SLOTS - 1)
